import numpy as np
import ml_dtypes

BF16 = ml_dtypes.bfloat16


def bf(x):
    return np.asarray(x, np.float32).astype(BF16)


def f32(x):
    return np.asarray(x, np.float32)


def f64(x):
    return np.asarray(x).astype(np.float64)


def striped(idx):
    return np.tile(idx.reshape(-1, 16).T, (8, 1))


C, S, N = 256, 4096, 1024
DOP, NOR, BIAS = 0.75, 0.5, 0.5


def sigmoid(v):
    return 1.0 / (1.0 + np.exp(-v))


def setup_inputs():
    return {
        "base": f32(np.random.standard_normal((C, S))),
        "x": bf(np.random.standard_normal((C, N))),
        "w_gate": bf(np.random.standard_normal((C, C)) / np.sqrt(C)),
        "b_gate": f32(BIAS * np.random.standard_normal((C, 1))),
        "w_filter": bf(np.random.standard_normal((C, C)) / np.sqrt(C)),
        "b_filter": f32(BIAS * np.random.standard_normal((C, 1))),
        "offs": striped(np.random.permutation(S)[:N]),
    }


def reference(base, x, w_gate, b_gate, w_filter, b_filter, offs):
    idx = offs[:16].T.reshape(-1)
    xs = f64(x)
    gate = sigmoid(f64(w_gate).T @ xs + f64(b_gate))
    x1 = xs * (1.0 + DOP * gate)
    noise = np.tanh(f64(w_filter).T @ x1 + f64(b_filter))
    out = f64(base).copy()
    out[:, idx] = x1 + NOR * noise
    return out

@@ -1,0 +1,92 @@
+import concourse.mybir as mybir
+
+F32 = mybir.dt.float32
+BF16 = mybir.dt.bfloat16
+U16 = mybir.dt.uint16
+ADD = mybir.AluOpType.add
+MULT = mybir.AluOpType.mult
+SIGMOID = mybir.ActivationFunctionType.Sigmoid
+TANH = mybir.ActivationFunctionType.Tanh
+
+P = 128
+C = 256
+S = 4096
+N = 1024
+BLOCKS = C // P
+BANK = 512
+PIECES = N // BANK
+
+DOPAMINE = 0.75
+NORADRENALINE = 0.5
+
+FLOPS = 2 * 2 * C * C * N
+
+
+def tile_opengrammarmodel_kernel(tc, base, x, w_gate, b_gate, w_filter, b_filter, offs, out):
+    nc = tc.nc
+    with (
+        tc.tile_pool(name="held", bufs=1) as held,
+        tc.tile_pool(name="work", bufs=3) as work,
+        tc.psum_pool(name="psum", bufs=4) as psum,
+    ):
+        gate_w = held.tile([P, BLOCKS, C], BF16, name="gate_w")
+        nc.sync.dma_start(gate_w[:], w_gate.rearrange("(kb p) c -> p kb c", p=P))
+        tokens = held.tile([P, BLOCKS, N], BF16, name="tokens")
+        nc.sync.dma_start(tokens[:], x.rearrange("(kb p) n -> p kb n", p=P))
+        filter_w = held.tile([P, BLOCKS, C], BF16, name="filter_w")
+        nc.sync.dma_start(filter_w[:], w_filter.rearrange("(kb p) c -> p kb c", p=P))
+        offsets = held.tile([P, N // 16], U16, name="offsets")
+        nc.sync.dma_start(offsets[:], offs)
+        gate_b = held.tile([P, BLOCKS], F32, name="gate_b")
+        filter_b = held.tile([P, BLOCKS], F32, name="filter_b")
+        with nc.allow_non_contiguous_dma(reason="one bias value to a partition"):
+            nc.scalar.dma_start(gate_b[:], b_gate.rearrange("(cb p) o -> p (cb o)", p=P))
+            nc.scalar.dma_start(filter_b[:], b_filter.rearrange("(cb p) o -> p (cb o)", p=P))
+        windows = []
+        for cb in range(BLOCKS):
+            window = held.tile([P, S], F32, name=f"window{cb}")
+            nc.sync.dma_start(window[:], base[cb * P : (cb + 1) * P, :])
+            windows.append(window)
+
+        amplified = held.tile([P, BLOCKS, N], F32, name="amplified")
+        for cb in range(BLOCKS):
+            nc.vector.tensor_scalar_mul(amplified[:, cb, :], tokens[:, cb, :], DOPAMINE)
+        x1 = held.tile([P, BLOCKS, N], F32, name="x1")
+        x1_bf = held.tile([P, BLOCKS, N], BF16, name="x1_bf")
+        for piece in range(PIECES):
+            cols = slice(piece * BANK, (piece + 1) * BANK)
+            for cb in range(BLOCKS):
+                gate_ps = psum.tile([P, BANK], F32, name="gate_ps")
+                for kb in range(BLOCKS):
+                    nc.tensor.matmul(
+                        gate_ps[:],
+                        gate_w[:, kb, cb * P : (cb + 1) * P],
+                        tokens[:, kb, cols],
+                        start=(kb == 0),
+                        stop=(kb == BLOCKS - 1),
+                    )
+                gate = work.tile([P, BANK], F32, name="gate")
+                nc.scalar.activation(gate[:], gate_ps[:], SIGMOID, bias=gate_b[:, cb : cb + 1])
+                nc.vector.scalar_tensor_tensor(
+                    x1[:, cb, cols], gate[:], 1.0 / DOPAMINE, amplified[:, cb, cols], ADD, MULT
+                )
+                nc.vector.tensor_copy(x1_bf[:, cb, cols], x1[:, cb, cols])
+
+        for cb in range(BLOCKS):
+            half_noise = held.tile([P, N], F32, name=f"half_noise{cb}")
+            for piece in range(PIECES):
+                cols = slice(piece * BANK, (piece + 1) * BANK)
+                noise_ps = psum.tile([P, BANK], F32, name="noise_ps")
+                for kb in range(BLOCKS):
+                    nc.tensor.matmul(
+                        noise_ps[:],
+                        filter_w[:, kb, cb * P : (cb + 1) * P],
+                        x1_bf[:, kb, cols],
+                        start=(kb == 0),
+                        stop=(kb == BLOCKS - 1),
+                    )
+                noise = work.tile([P, BANK], F32, name="noise")
+                nc.scalar.activation(noise[:], noise_ps[:], TANH, bias=filter_b[:, cb : cb + 1])
+                nc.vector.tensor_scalar_mul(half_noise[:, cols], noise[:], NORADRENALINE)
+            nc.vector.tensor_tensor(windows[cb][:].indirect(offsets[:]), x1[:, cb, :], half_noise[:], ADD)
+            nc.sync.dma_start(out[cb * P : (cb + 1) * P, :], windows[cb][:])

@@ -26,13 +26,16 @@ def tile_opengrammarmodel_kernel(tc, base, x, w_gate, b_gate, w_filter, b_filter
     nc = tc.nc
     with (
         tc.tile_pool(name="held", bufs=1) as held,
-        tc.tile_pool(name="work", bufs=3) as work,
+        tc.tile_pool(name="work", bufs=2) as work,
         tc.psum_pool(name="psum", bufs=4) as psum,
     ):
         gate_w = held.tile([P, BLOCKS, C], BF16, name="gate_w")
         nc.sync.dma_start(gate_w[:], w_gate.rearrange("(kb p) c -> p kb c", p=P))
         tokens = held.tile([P, BLOCKS, N], BF16, name="tokens")
-        nc.sync.dma_start(tokens[:], x.rearrange("(kb p) n -> p kb n", p=P))
+        x_blocks = x.rearrange("(kb p) n -> p kb n", p=P)
+        for piece in range(PIECES):
+            cols = slice(piece * BANK, (piece + 1) * BANK)
+            nc.sync.dma_start(tokens[:, :, cols], x_blocks[:, :, cols])
         filter_w = held.tile([P, BLOCKS, C], BF16, name="filter_w")
         nc.sync.dma_start(filter_w[:], w_filter.rearrange("(kb p) c -> p kb c", p=P))
         offsets = held.tile([P, N // 16], U16, name="offsets")
@@ -49,12 +52,11 @@ def tile_opengrammarmodel_kernel(tc, base, x, w_gate, b_gate, w_filter, b_filter
             windows.append(window)
 
         amplified = held.tile([P, BLOCKS, N], F32, name="amplified")
-        for cb in range(BLOCKS):
-            nc.vector.tensor_scalar_mul(amplified[:, cb, :], tokens[:, cb, :], DOPAMINE)
-        x1 = held.tile([P, BLOCKS, N], F32, name="x1")
+        gate = held.tile([P, BLOCKS, N], F32, name="gate")
         x1_bf = held.tile([P, BLOCKS, N], BF16, name="x1_bf")
         for piece in range(PIECES):
             cols = slice(piece * BANK, (piece + 1) * BANK)
+            nc.vector.tensor_scalar_mul(amplified[:, :, cols], tokens[:, :, cols], DOPAMINE)
             for cb in range(BLOCKS):
                 gate_ps = psum.tile([P, BANK], F32, name="gate_ps")
                 for kb in range(BLOCKS):
@@ -65,15 +67,13 @@ def tile_opengrammarmodel_kernel(tc, base, x, w_gate, b_gate, w_filter, b_filter
                         start=(kb == 0),
                         stop=(kb == BLOCKS - 1),
                     )
-                gate = work.tile([P, BANK], F32, name="gate")
-                nc.scalar.activation(gate[:], gate_ps[:], SIGMOID, bias=gate_b[:, cb : cb + 1])
+                nc.scalar.activation(gate[:, cb, cols], gate_ps[:], SIGMOID, bias=gate_b[:, cb : cb + 1])
                 nc.vector.scalar_tensor_tensor(
-                    x1[:, cb, cols], gate[:], 1.0 / DOPAMINE, amplified[:, cb, cols], ADD, MULT
+                    x1_bf[:, cb, cols], gate[:, cb, cols], 1.0 / DOPAMINE, amplified[:, cb, cols], ADD, MULT
                 )
-                nc.vector.tensor_copy(x1_bf[:, cb, cols], x1[:, cb, cols])
 
         for cb in range(BLOCKS):
-            half_noise = held.tile([P, N], F32, name=f"half_noise{cb}")
+            noise = work.tile([P, N], F32, name="noise")
             for piece in range(PIECES):
                 cols = slice(piece * BANK, (piece + 1) * BANK)
                 noise_ps = psum.tile([P, BANK], F32, name="noise_ps")
@@ -85,8 +85,15 @@ def tile_opengrammarmodel_kernel(tc, base, x, w_gate, b_gate, w_filter, b_filter
                         start=(kb == 0),
                         stop=(kb == BLOCKS - 1),
                     )
-                noise = work.tile([P, BANK], F32, name="noise")
-                nc.scalar.activation(noise[:], noise_ps[:], TANH, bias=filter_b[:, cb : cb + 1])
-                nc.vector.tensor_scalar_mul(half_noise[:, cols], noise[:], NORADRENALINE)
-            nc.vector.tensor_tensor(windows[cb][:].indirect(offsets[:]), x1[:, cb, :], half_noise[:], ADD)
+                nc.scalar.activation(noise[:, cols], noise_ps[:], TANH, bias=filter_b[:, cb : cb + 1])
+            x1 = work.tile([P, N], F32, name="x1")
+            nc.vector.scalar_tensor_tensor(
+                x1[:], gate[:, cb, :], 1.0 / DOPAMINE, amplified[:, cb, :], ADD, MULT
+            )
+            half_noise = work.tile([P, N], F32, name="half_noise")
+            if cb == 0:
+                nc.vector.tensor_scalar_mul(half_noise[:], noise[:], NORADRENALINE)
+            else:
+                nc.scalar.mul(half_noise[:], noise[:], NORADRENALINE)
+            nc.vector.tensor_tensor(windows[cb][:].indirect(offsets[:]), x1[:], half_noise[:], ADD)
             nc.sync.dma_start(out[cb * P : (cb + 1) * P, :], windows[cb][:])

@@ -15,6 +15,7 @@ N = 1024
 BLOCKS = C // P
 BANK = 512
 PIECES = N // BANK
+WARM_MATMULS = 6
 
 DOPAMINE = 0.75
 NORADRENALINE = 0.5
@@ -27,8 +28,17 @@ def tile_opengrammarmodel_kernel(tc, base, x, w_gate, b_gate, w_filter, b_filter
     with (
         tc.tile_pool(name="held", bufs=1) as held,
         tc.tile_pool(name="work", bufs=2) as work,
-        tc.psum_pool(name="psum", bufs=4) as psum,
+        tc.psum_pool(name="psum", bufs=3) as psum,
+        tc.psum_pool(name="warm", bufs=1) as warm,
     ):
+        zeros = held.tile([P, BANK], BF16, name="zeros")
+        nc.vector.memset(zeros[:], 0.0)
+        warm_ps = warm.tile([P, BANK], F32, name="warm_ps")
+        for rep in range(WARM_MATMULS):
+            nc.tensor.matmul(warm_ps[:], zeros[:, 0:P], zeros[:], start=True, stop=True)
+        warm_gate = held.tile([P, 1], F32, name="warm_gate")
+        nc.scalar.activation(warm_gate[:], zeros[:, 0:1], SIGMOID)
+
         gate_w = held.tile([P, BLOCKS, C], BF16, name="gate_w")
         nc.sync.dma_start(gate_w[:], w_gate.rearrange("(kb p) c -> p kb c", p=P))
         tokens = held.tile([P, BLOCKS, N], BF16, name="tokens")

@@ -15,7 +15,7 @@ N = 1024
 BLOCKS = C // P
 BANK = 512
 PIECES = N // BANK
-WARM_MATMULS = 6
+WARM_MATMULS = 16
 
 DOPAMINE = 0.75
 NORADRENALINE = 0.5
@@ -31,11 +31,11 @@ def tile_opengrammarmodel_kernel(tc, base, x, w_gate, b_gate, w_filter, b_filter
         tc.psum_pool(name="psum", bufs=3) as psum,
         tc.psum_pool(name="warm", bufs=1) as warm,
     ):
-        zeros = held.tile([P, BANK], BF16, name="zeros")
+        zeros = held.tile([P, P], BF16, name="zeros")
         nc.vector.memset(zeros[:], 0.0)
-        warm_ps = warm.tile([P, BANK], F32, name="warm_ps")
+        warm_ps = warm.tile([P, P], F32, name="warm_ps")
         for rep in range(WARM_MATMULS):
-            nc.tensor.matmul(warm_ps[:], zeros[:, 0:P], zeros[:], start=True, stop=True)
+            nc.tensor.matmul(warm_ps[:], zeros[:], zeros[:], start=True, stop=True)
         warm_gate = held.tile([P, 1], F32, name="warm_gate")
         nc.scalar.activation(warm_gate[:], zeros[:, 0:1], SIGMOID)
 

@@ -7,6 +7,7 @@ ADD = mybir.AluOpType.add
 MULT = mybir.AluOpType.mult
 SIGMOID = mybir.ActivationFunctionType.Sigmoid
 TANH = mybir.ActivationFunctionType.Tanh
+COPY = mybir.ActivationFunctionType.Copy
 
 P = 128
 C = 256
@@ -15,7 +16,7 @@ N = 1024
 BLOCKS = C // P
 BANK = 512
 PIECES = N // BANK
-WARM_MATMULS = 16
+WARM_MATMULS = 12
 
 DOPAMINE = 0.75
 NORADRENALINE = 0.5
@@ -62,11 +63,13 @@ def tile_opengrammarmodel_kernel(tc, base, x, w_gate, b_gate, w_filter, b_filter
             windows.append(window)
 
         amplified = held.tile([P, BLOCKS, N], F32, name="amplified")
+        for piece in range(PIECES):
+            cols = slice(piece * BANK, (piece + 1) * BANK)
+            nc.vector.tensor_scalar_mul(amplified[:, :, cols], tokens[:, :, cols], DOPAMINE)
         gate = held.tile([P, BLOCKS, N], F32, name="gate")
         x1_bf = held.tile([P, BLOCKS, N], BF16, name="x1_bf")
         for piece in range(PIECES):
             cols = slice(piece * BANK, (piece + 1) * BANK)
-            nc.vector.tensor_scalar_mul(amplified[:, :, cols], tokens[:, :, cols], DOPAMINE)
             for cb in range(BLOCKS):
                 gate_ps = psum.tile([P, BANK], F32, name="gate_ps")
                 for kb in range(BLOCKS):
@@ -83,7 +86,18 @@ def tile_opengrammarmodel_kernel(tc, base, x, w_gate, b_gate, w_filter, b_filter
                 )
 
         for cb in range(BLOCKS):
+            first = cb == 0
+            x1 = work.tile([P, N], F32, name="x1")
+            if first:
+                nc.vector.scalar_tensor_tensor(
+                    x1[:], gate[:, cb, :], 1.0 / DOPAMINE, amplified[:, cb, :], ADD, MULT
+                )
+            else:
+                boost = work.tile([P, N], F32, name="boost")
+                nc.scalar.activation(boost[:], gate[:, cb, :], COPY, bias=1.0, scale=DOPAMINE)
+                nc.gpsimd.tensor_tensor(x1[:], boost[:], tokens[:, cb, :], MULT)
             noise = work.tile([P, N], F32, name="noise")
+            half_noise = work.tile([P, N], F32, name="half_noise")
             for piece in range(PIECES):
                 cols = slice(piece * BANK, (piece + 1) * BANK)
                 noise_ps = psum.tile([P, BANK], F32, name="noise_ps")
@@ -96,14 +110,9 @@ def tile_opengrammarmodel_kernel(tc, base, x, w_gate, b_gate, w_filter, b_filter
                         stop=(kb == BLOCKS - 1),
                     )
                 nc.scalar.activation(noise[:, cols], noise_ps[:], TANH, bias=filter_b[:, cb : cb + 1])
-            x1 = work.tile([P, N], F32, name="x1")
-            nc.vector.scalar_tensor_tensor(
-                x1[:], gate[:, cb, :], 1.0 / DOPAMINE, amplified[:, cb, :], ADD, MULT
-            )
-            half_noise = work.tile([P, N], F32, name="half_noise")
-            if cb == 0:
-                nc.vector.tensor_scalar_mul(half_noise[:], noise[:], NORADRENALINE)
-            else:
-                nc.scalar.mul(half_noise[:], noise[:], NORADRENALINE)
+                if first:
+                    nc.vector.tensor_scalar_mul(half_noise[:, cols], noise[:, cols], NORADRENALINE)
+                else:
+                    nc.scalar.mul(half_noise[:, cols], noise[:, cols], NORADRENALINE)
             nc.vector.tensor_tensor(windows[cb][:].indirect(offsets[:]), x1[:], half_noise[:], ADD)
             nc.sync.dma_start(out[cb * P : (cb + 1) * P, :], windows[cb][:])

@@ -7,16 +7,16 @@ ADD = mybir.AluOpType.add
 MULT = mybir.AluOpType.mult
 SIGMOID = mybir.ActivationFunctionType.Sigmoid
 TANH = mybir.ActivationFunctionType.Tanh
-COPY = mybir.ActivationFunctionType.Copy
 
 P = 128
 C = 256
 S = 4096
 N = 1024
 BLOCKS = C // P
-BANK = 512
-PIECES = N // BANK
-WARM_MATMULS = 12
+HALVES = 2
+PIECE = 256
+PIECES = N // PIECE
+WARM_MATMULS = 16
 
 DOPAMINE = 0.75
 NORADRENALINE = 0.5
@@ -28,50 +28,53 @@ def tile_opengrammarmodel_kernel(tc, base, x, w_gate, b_gate, w_filter, b_filter
     nc = tc.nc
     with (
         tc.tile_pool(name="held", bufs=1) as held,
-        tc.tile_pool(name="work", bufs=2) as work,
+        tc.tile_pool(name="turn", bufs=1) as turn,
+        tc.tile_pool(name="ring", bufs=3) as ring,
         tc.psum_pool(name="psum", bufs=3) as psum,
-        tc.psum_pool(name="warm", bufs=1) as warm,
+        tc.psum_pool(name="once", bufs=1) as once,
     ):
-        zeros = held.tile([P, P], BF16, name="zeros")
-        nc.vector.memset(zeros[:], 0.0)
-        warm_ps = warm.tile([P, P], F32, name="warm_ps")
-        for rep in range(WARM_MATMULS):
-            nc.tensor.matmul(warm_ps[:], zeros[:], zeros[:], start=True, stop=True)
-        warm_gate = held.tile([P, 1], F32, name="warm_gate")
-        nc.scalar.activation(warm_gate[:], zeros[:, 0:1], SIGMOID)
-
         gate_w = held.tile([P, BLOCKS, C], BF16, name="gate_w")
         nc.sync.dma_start(gate_w[:], w_gate.rearrange("(kb p) c -> p kb c", p=P))
         tokens = held.tile([P, BLOCKS, N], BF16, name="tokens")
         x_blocks = x.rearrange("(kb p) n -> p kb n", p=P)
-        for piece in range(PIECES):
-            cols = slice(piece * BANK, (piece + 1) * BANK)
+        gate_b = held.tile([P, BLOCKS], F32, name="gate_b")
+        for half in range(HALVES):
+            cols = slice(half * (N // HALVES), (half + 1) * (N // HALVES))
             nc.sync.dma_start(tokens[:, :, cols], x_blocks[:, :, cols])
+            if half == 0:
+                with nc.allow_non_contiguous_dma(reason="one bias value to a partition"):
+                    nc.sync.dma_start(gate_b[:], b_gate.rearrange("(cb p) o -> p (cb o)", p=P))
         filter_w = held.tile([P, BLOCKS, C], BF16, name="filter_w")
         nc.sync.dma_start(filter_w[:], w_filter.rearrange("(kb p) c -> p kb c", p=P))
         offsets = held.tile([P, N // 16], U16, name="offsets")
         nc.sync.dma_start(offsets[:], offs)
-        gate_b = held.tile([P, BLOCKS], F32, name="gate_b")
         filter_b = held.tile([P, BLOCKS], F32, name="filter_b")
         with nc.allow_non_contiguous_dma(reason="one bias value to a partition"):
-            nc.scalar.dma_start(gate_b[:], b_gate.rearrange("(cb p) o -> p (cb o)", p=P))
-            nc.scalar.dma_start(filter_b[:], b_filter.rearrange("(cb p) o -> p (cb o)", p=P))
+            nc.sync.dma_start(filter_b[:], b_filter.rearrange("(cb p) o -> p (cb o)", p=P))
         windows = []
         for cb in range(BLOCKS):
             window = held.tile([P, S], F32, name=f"window{cb}")
             nc.sync.dma_start(window[:], base[cb * P : (cb + 1) * P, :])
             windows.append(window)
 
+        zeros = held.tile([P, P], BF16, name="zeros")
+        nc.vector.memset(zeros[:], 0.0)
+        warm_ps = once.tile([P, P], F32, name="warm_ps")
+        for rep in range(WARM_MATMULS):
+            nc.tensor.matmul(warm_ps[:], zeros[:], zeros[:], start=True, stop=True)
+        warm_gate = held.tile([P, 1], F32, name="warm_gate")
+        nc.scalar.activation(warm_gate[:], zeros[:, 0:1], SIGMOID)
+
         amplified = held.tile([P, BLOCKS, N], F32, name="amplified")
-        for piece in range(PIECES):
-            cols = slice(piece * BANK, (piece + 1) * BANK)
+        for half in range(HALVES):
+            cols = slice(half * (N // HALVES), (half + 1) * (N // HALVES))
             nc.vector.tensor_scalar_mul(amplified[:, :, cols], tokens[:, :, cols], DOPAMINE)
-        gate = held.tile([P, BLOCKS, N], F32, name="gate")
+        x1 = held.tile([P, BLOCKS, N], F32, name="x1")
         x1_bf = held.tile([P, BLOCKS, N], BF16, name="x1_bf")
         for piece in range(PIECES):
-            cols = slice(piece * BANK, (piece + 1) * BANK)
+            cols = slice(piece * PIECE, (piece + 1) * PIECE)
             for cb in range(BLOCKS):
-                gate_ps = psum.tile([P, BANK], F32, name="gate_ps")
+                gate_ps = psum.tile([P, PIECE], F32, name="gate_ps")
                 for kb in range(BLOCKS):
                     nc.tensor.matmul(
                         gate_ps[:],
@@ -80,27 +83,19 @@ def tile_opengrammarmodel_kernel(tc, base, x, w_gate, b_gate, w_filter, b_filter
                         start=(kb == 0),
                         stop=(kb == BLOCKS - 1),
                     )
-                nc.scalar.activation(gate[:, cb, cols], gate_ps[:], SIGMOID, bias=gate_b[:, cb : cb + 1])
+                gate = ring.tile([P, PIECE], F32, name="gate")
+                nc.scalar.activation(gate[:], gate_ps[:], SIGMOID, bias=gate_b[:, cb : cb + 1])
                 nc.vector.scalar_tensor_tensor(
-                    x1_bf[:, cb, cols], gate[:, cb, cols], 1.0 / DOPAMINE, amplified[:, cb, cols], ADD, MULT
+                    x1[:, cb, cols], gate[:], 1.0 / DOPAMINE, amplified[:, cb, cols], ADD, MULT
                 )
+                nc.vector.tensor_copy(x1_bf[:, cb, cols], x1[:, cb, cols])
 
+        half_noise = held.tile([P, BLOCKS, N], F32, name="half_noise")
         for cb in range(BLOCKS):
-            first = cb == 0
-            x1 = work.tile([P, N], F32, name="x1")
-            if first:
-                nc.vector.scalar_tensor_tensor(
-                    x1[:], gate[:, cb, :], 1.0 / DOPAMINE, amplified[:, cb, :], ADD, MULT
-                )
-            else:
-                boost = work.tile([P, N], F32, name="boost")
-                nc.scalar.activation(boost[:], gate[:, cb, :], COPY, bias=1.0, scale=DOPAMINE)
-                nc.gpsimd.tensor_tensor(x1[:], boost[:], tokens[:, cb, :], MULT)
-            noise = work.tile([P, N], F32, name="noise")
-            half_noise = work.tile([P, N], F32, name="half_noise")
+            noise = turn.tile([P, N], F32, name="noise")
             for piece in range(PIECES):
-                cols = slice(piece * BANK, (piece + 1) * BANK)
-                noise_ps = psum.tile([P, BANK], F32, name="noise_ps")
+                cols = slice(piece * PIECE, (piece + 1) * PIECE)
+                noise_ps = psum.tile([P, PIECE], F32, name="noise_ps")
                 for kb in range(BLOCKS):
                     nc.tensor.matmul(
                         noise_ps[:],
@@ -110,9 +105,9 @@ def tile_opengrammarmodel_kernel(tc, base, x, w_gate, b_gate, w_filter, b_filter
                         stop=(kb == BLOCKS - 1),
                     )
                 nc.scalar.activation(noise[:, cols], noise_ps[:], TANH, bias=filter_b[:, cb : cb + 1])
-                if first:
-                    nc.vector.tensor_scalar_mul(half_noise[:, cols], noise[:, cols], NORADRENALINE)
+                if cb == 0:
+                    nc.vector.tensor_scalar_mul(half_noise[:, cb, cols], noise[:, cols], NORADRENALINE)
                 else:
-                    nc.scalar.mul(half_noise[:, cols], noise[:, cols], NORADRENALINE)
-            nc.vector.tensor_tensor(windows[cb][:].indirect(offsets[:]), x1[:], half_noise[:], ADD)
+                    nc.scalar.mul(half_noise[:, cb, cols], noise[:, cols], NORADRENALINE)
+            nc.vector.tensor_tensor(windows[cb][:].indirect(offsets[:]), x1[:, cb, :], half_noise[:, cb, :], ADD)
             nc.sync.dma_start(out[cb * P : (cb + 1) * P, :], windows[cb][:])

@@ -29,32 +29,31 @@ def tile_opengrammarmodel_kernel(tc, base, x, w_gate, b_gate, w_filter, b_filter
     with (
         tc.tile_pool(name="held", bufs=1) as held,
         tc.tile_pool(name="turn", bufs=1) as turn,
-        tc.tile_pool(name="ring", bufs=3) as ring,
         tc.psum_pool(name="psum", bufs=3) as psum,
         tc.psum_pool(name="once", bufs=1) as once,
     ):
-        gate_w = held.tile([P, BLOCKS, C], BF16, name="gate_w")
-        nc.sync.dma_start(gate_w[:], w_gate.rearrange("(kb p) c -> p kb c", p=P))
+        gate_w = held.tile([P, BLOCKS, P, BLOCKS], BF16, name="gate_w")
+        nc.sync.dma_start(gate_w[:], w_gate.rearrange("(p kb) (m cb) -> p kb m cb", kb=BLOCKS, cb=BLOCKS))
         tokens = held.tile([P, BLOCKS, N], BF16, name="tokens")
-        x_blocks = x.rearrange("(kb p) n -> p kb n", p=P)
+        x_blocks = x.rearrange("(p kb) n -> p kb n", kb=BLOCKS)
         gate_b = held.tile([P, BLOCKS], F32, name="gate_b")
         for half in range(HALVES):
             cols = slice(half * (N // HALVES), (half + 1) * (N // HALVES))
             nc.sync.dma_start(tokens[:, :, cols], x_blocks[:, :, cols])
             if half == 0:
-                with nc.allow_non_contiguous_dma(reason="one bias value to a partition"):
-                    nc.sync.dma_start(gate_b[:], b_gate.rearrange("(cb p) o -> p (cb o)", p=P))
-        filter_w = held.tile([P, BLOCKS, C], BF16, name="filter_w")
-        nc.sync.dma_start(filter_w[:], w_filter.rearrange("(kb p) c -> p kb c", p=P))
+                nc.sync.dma_start(gate_b[:], b_gate.rearrange("(p cb) o -> p (cb o)", cb=BLOCKS))
+        filter_w = held.tile([P, BLOCKS, P, BLOCKS], BF16, name="filter_w")
+        nc.sync.dma_start(filter_w[:], w_filter.rearrange("(p kb) (m cb) -> p kb m cb", kb=BLOCKS, cb=BLOCKS))
         offsets = held.tile([P, N // 16], U16, name="offsets")
         nc.sync.dma_start(offsets[:], offs)
         filter_b = held.tile([P, BLOCKS], F32, name="filter_b")
-        with nc.allow_non_contiguous_dma(reason="one bias value to a partition"):
-            nc.sync.dma_start(filter_b[:], b_filter.rearrange("(cb p) o -> p (cb o)", p=P))
+        nc.sync.dma_start(filter_b[:], b_filter.rearrange("(p cb) o -> p (cb o)", cb=BLOCKS))
+        base_blocks = base.rearrange("(p cb) s -> p cb s", cb=BLOCKS)
+        out_blocks = out.rearrange("(p cb) s -> p cb s", cb=BLOCKS)
         windows = []
         for cb in range(BLOCKS):
             window = held.tile([P, S], F32, name=f"window{cb}")
-            nc.sync.dma_start(window[:], base[cb * P : (cb + 1) * P, :])
+            nc.sync.dma_start(window[:], base_blocks[:, cb, :])
             windows.append(window)
 
         zeros = held.tile([P, P], BF16, name="zeros")
@@ -69,7 +68,7 @@ def tile_opengrammarmodel_kernel(tc, base, x, w_gate, b_gate, w_filter, b_filter
         for half in range(HALVES):
             cols = slice(half * (N // HALVES), (half + 1) * (N // HALVES))
             nc.vector.tensor_scalar_mul(amplified[:, :, cols], tokens[:, :, cols], DOPAMINE)
-        x1 = held.tile([P, BLOCKS, N], F32, name="x1")
+        gate = held.tile([P, BLOCKS, N], F32, name="gate")
         x1_bf = held.tile([P, BLOCKS, N], BF16, name="x1_bf")
         for piece in range(PIECES):
             cols = slice(piece * PIECE, (piece + 1) * PIECE)
@@ -78,17 +77,22 @@ def tile_opengrammarmodel_kernel(tc, base, x, w_gate, b_gate, w_filter, b_filter
                 for kb in range(BLOCKS):
                     nc.tensor.matmul(
                         gate_ps[:],
-                        gate_w[:, kb, cb * P : (cb + 1) * P],
+                        gate_w[:, kb, :, cb],
                         tokens[:, kb, cols],
                         start=(kb == 0),
                         stop=(kb == BLOCKS - 1),
                     )
-                gate = ring.tile([P, PIECE], F32, name="gate")
-                nc.scalar.activation(gate[:], gate_ps[:], SIGMOID, bias=gate_b[:, cb : cb + 1])
+                nc.scalar.activation(gate[:, cb, cols], gate_ps[:], SIGMOID, bias=gate_b[:, cb : cb + 1])
                 nc.vector.scalar_tensor_tensor(
-                    x1[:, cb, cols], gate[:], 1.0 / DOPAMINE, amplified[:, cb, cols], ADD, MULT
+                    x1_bf[:, cb, cols], gate[:, cb, cols], 1.0 / DOPAMINE, amplified[:, cb, cols], ADD, MULT
                 )
-                nc.vector.tensor_copy(x1_bf[:, cb, cols], x1[:, cb, cols])
+        x1 = held.tile([P, BLOCKS, N], F32, name="x1")
+        for cb in range(BLOCKS):
+            for piece in range(PIECES):
+                cols = slice(piece * PIECE, (piece + 1) * PIECE)
+                nc.vector.scalar_tensor_tensor(
+                    x1[:, cb, cols], gate[:, cb, cols], 1.0 / DOPAMINE, amplified[:, cb, cols], ADD, MULT
+                )
 
         half_noise = held.tile([P, BLOCKS, N], F32, name="half_noise")
         for cb in range(BLOCKS):
@@ -99,15 +103,12 @@ def tile_opengrammarmodel_kernel(tc, base, x, w_gate, b_gate, w_filter, b_filter
                 for kb in range(BLOCKS):
                     nc.tensor.matmul(
                         noise_ps[:],
-                        filter_w[:, kb, cb * P : (cb + 1) * P],
+                        filter_w[:, kb, :, cb],
                         x1_bf[:, kb, cols],
                         start=(kb == 0),
                         stop=(kb == BLOCKS - 1),
                     )
                 nc.scalar.activation(noise[:, cols], noise_ps[:], TANH, bias=filter_b[:, cb : cb + 1])
-                if cb == 0:
-                    nc.vector.tensor_scalar_mul(half_noise[:, cb, cols], noise[:, cols], NORADRENALINE)
-                else:
-                    nc.scalar.mul(half_noise[:, cb, cols], noise[:, cols], NORADRENALINE)
+                nc.scalar.mul(half_noise[:, cb, cols], noise[:, cols], NORADRENALINE)
             nc.vector.tensor_tensor(windows[cb][:].indirect(offsets[:]), x1[:, cb, :], half_noise[:, cb, :], ADD)
-            nc.sync.dma_start(out[cb * P : (cb + 1) * P, :], windows[cb][:])
+            nc.sync.dma_start(out_blocks[:, cb, :], windows[cb][:])

@@ -13,7 +13,6 @@ C = 256
 S = 4096
 N = 1024
 BLOCKS = C // P
-HALVES = 2
 PIECE = 256
 PIECES = N // PIECE
 WARM_MATMULS = 16
@@ -37,10 +36,10 @@ def tile_opengrammarmodel_kernel(tc, base, x, w_gate, b_gate, w_filter, b_filter
         tokens = held.tile([P, BLOCKS, N], BF16, name="tokens")
         x_blocks = x.rearrange("(p kb) n -> p kb n", kb=BLOCKS)
         gate_b = held.tile([P, BLOCKS], F32, name="gate_b")
-        for half in range(HALVES):
-            cols = slice(half * (N // HALVES), (half + 1) * (N // HALVES))
+        for piece in range(PIECES):
+            cols = slice(piece * PIECE, (piece + 1) * PIECE)
             nc.sync.dma_start(tokens[:, :, cols], x_blocks[:, :, cols])
-            if half == 0:
+            if piece == 0:
                 nc.sync.dma_start(gate_b[:], b_gate.rearrange("(p cb) o -> p (cb o)", cb=BLOCKS))
         filter_w = held.tile([P, BLOCKS, P, BLOCKS], BF16, name="filter_w")
         nc.sync.dma_start(filter_w[:], w_filter.rearrange("(p kb) (m cb) -> p kb m cb", kb=BLOCKS, cb=BLOCKS))
@@ -65,8 +64,8 @@ def tile_opengrammarmodel_kernel(tc, base, x, w_gate, b_gate, w_filter, b_filter
         nc.scalar.activation(warm_gate[:], zeros[:, 0:1], SIGMOID)
 
         amplified = held.tile([P, BLOCKS, N], F32, name="amplified")
-        for half in range(HALVES):
-            cols = slice(half * (N // HALVES), (half + 1) * (N // HALVES))
+        for piece in range(PIECES):
+            cols = slice(piece * PIECE, (piece + 1) * PIECE)
             nc.vector.tensor_scalar_mul(amplified[:, :, cols], tokens[:, :, cols], DOPAMINE)
         gate = held.tile([P, BLOCKS, N], F32, name="gate")
         x1_bf = held.tile([P, BLOCKS, N], BF16, name="x1_bf")
@@ -111,4 +110,5 @@ def tile_opengrammarmodel_kernel(tc, base, x, w_gate, b_gate, w_filter, b_filter
                 nc.scalar.activation(noise[:, cols], noise_ps[:], TANH, bias=filter_b[:, cb : cb + 1])
                 nc.scalar.mul(half_noise[:, cb, cols], noise[:, cols], NORADRENALINE)
             nc.vector.tensor_tensor(windows[cb][:].indirect(offsets[:]), x1[:, cb, :], half_noise[:, cb, :], ADD)
-            nc.sync.dma_start(out_blocks[:, cb, :], windows[cb][:])
+            nc.sync.dma_start(out_blocks[:, cb, 0 : S // 2], windows[cb][:, 0 : S // 2])
+            nc.scalar.dma_start(out_blocks[:, cb, S // 2 : S], windows[cb][:, S // 2 : S])

@@ -15,7 +15,7 @@ N = 1024
 BLOCKS = C // P
 PIECE = 256
 PIECES = N // PIECE
-WARM_MATMULS = 16
+WARM_MATMULS = 14
 
 DOPAMINE = 0.75
 NORADRENALINE = 0.5

@@ -14,7 +14,8 @@ S = 4096
 N = 1024
 BLOCKS = C // P
 PIECE = 256
-PIECES = N // PIECE
+WIDTHS = [PIECE // 2] + (N // PIECE - 1) * [PIECE] + [PIECE // 2]
+PIECE_COLS = [slice(sum(WIDTHS[:piece]), sum(WIDTHS[: piece + 1])) for piece in range(len(WIDTHS))]
 WARM_MATMULS = 14
 
 DOPAMINE = 0.75
@@ -36,8 +37,7 @@ def tile_opengrammarmodel_kernel(tc, base, x, w_gate, b_gate, w_filter, b_filter
         tokens = held.tile([P, BLOCKS, N], BF16, name="tokens")
         x_blocks = x.rearrange("(p kb) n -> p kb n", kb=BLOCKS)
         gate_b = held.tile([P, BLOCKS], F32, name="gate_b")
-        for piece in range(PIECES):
-            cols = slice(piece * PIECE, (piece + 1) * PIECE)
+        for piece, cols in enumerate(PIECE_COLS):
             nc.sync.dma_start(tokens[:, :, cols], x_blocks[:, :, cols])
             if piece == 0:
                 nc.sync.dma_start(gate_b[:], b_gate.rearrange("(p cb) o -> p (cb o)", cb=BLOCKS))
@@ -64,31 +64,29 @@ def tile_opengrammarmodel_kernel(tc, base, x, w_gate, b_gate, w_filter, b_filter
         nc.scalar.activation(warm_gate[:], zeros[:, 0:1], SIGMOID)
 
         amplified = held.tile([P, BLOCKS, N], F32, name="amplified")
-        for piece in range(PIECES):
-            cols = slice(piece * PIECE, (piece + 1) * PIECE)
+        for cols in PIECE_COLS:
             nc.vector.tensor_scalar_mul(amplified[:, :, cols], tokens[:, :, cols], DOPAMINE)
         gate = held.tile([P, BLOCKS, N], F32, name="gate")
         x1_bf = held.tile([P, BLOCKS, N], BF16, name="x1_bf")
-        for piece in range(PIECES):
-            cols = slice(piece * PIECE, (piece + 1) * PIECE)
+        for cols in PIECE_COLS:
+            width = cols.stop - cols.start
             for cb in range(BLOCKS):
                 gate_ps = psum.tile([P, PIECE], F32, name="gate_ps")
                 for kb in range(BLOCKS):
                     nc.tensor.matmul(
-                        gate_ps[:],
+                        gate_ps[:, 0:width],
                         gate_w[:, kb, :, cb],
                         tokens[:, kb, cols],
                         start=(kb == 0),
                         stop=(kb == BLOCKS - 1),
                     )
-                nc.scalar.activation(gate[:, cb, cols], gate_ps[:], SIGMOID, bias=gate_b[:, cb : cb + 1])
+                nc.scalar.activation(gate[:, cb, cols], gate_ps[:, 0:width], SIGMOID, bias=gate_b[:, cb : cb + 1])
                 nc.vector.scalar_tensor_tensor(
                     x1_bf[:, cb, cols], gate[:, cb, cols], 1.0 / DOPAMINE, amplified[:, cb, cols], ADD, MULT
                 )
         x1 = held.tile([P, BLOCKS, N], F32, name="x1")
         for cb in range(BLOCKS):
-            for piece in range(PIECES):
-                cols = slice(piece * PIECE, (piece + 1) * PIECE)
+            for cols in PIECE_COLS:
                 nc.vector.scalar_tensor_tensor(
                     x1[:, cb, cols], gate[:, cb, cols], 1.0 / DOPAMINE, amplified[:, cb, cols], ADD, MULT
                 )
@@ -96,18 +94,18 @@ def tile_opengrammarmodel_kernel(tc, base, x, w_gate, b_gate, w_filter, b_filter
         half_noise = held.tile([P, BLOCKS, N], F32, name="half_noise")
         for cb in range(BLOCKS):
             noise = turn.tile([P, N], F32, name="noise")
-            for piece in range(PIECES):
-                cols = slice(piece * PIECE, (piece + 1) * PIECE)
+            for cols in PIECE_COLS:
+                width = cols.stop - cols.start
                 noise_ps = psum.tile([P, PIECE], F32, name="noise_ps")
                 for kb in range(BLOCKS):
                     nc.tensor.matmul(
-                        noise_ps[:],
+                        noise_ps[:, 0:width],
                         filter_w[:, kb, :, cb],
                         x1_bf[:, kb, cols],
                         start=(kb == 0),
                         stop=(kb == BLOCKS - 1),
                     )
-                nc.scalar.activation(noise[:, cols], noise_ps[:], TANH, bias=filter_b[:, cb : cb + 1])
+                nc.scalar.activation(noise[:, cols], noise_ps[:, 0:width], TANH, bias=filter_b[:, cb : cb + 1])
                 nc.scalar.mul(half_noise[:, cb, cols], noise[:, cols], NORADRENALINE)
             nc.vector.tensor_tensor(windows[cb][:].indirect(offsets[:]), x1[:, cb, :], half_noise[:, cb, :], ADD)
             nc.sync.dma_start(out_blocks[:, cb, 0 : S // 2], windows[cb][:, 0 : S // 2])

@@ -32,21 +32,20 @@ def tile_opengrammarmodel_kernel(tc, base, x, w_gate, b_gate, w_filter, b_filter
         tc.psum_pool(name="psum", bufs=3) as psum,
         tc.psum_pool(name="once", bufs=1) as once,
     ):
+        gate_b = held.tile([P, BLOCKS], F32, name="gate_b")
+        nc.scalar.dma_start(gate_b[:], b_gate.rearrange("(p cb) o -> p (cb o)", cb=BLOCKS))
+        filter_b = held.tile([P, BLOCKS], F32, name="filter_b")
+        nc.scalar.dma_start(filter_b[:], b_filter.rearrange("(p cb) o -> p (cb o)", cb=BLOCKS))
         gate_w = held.tile([P, BLOCKS, P, BLOCKS], BF16, name="gate_w")
         nc.sync.dma_start(gate_w[:], w_gate.rearrange("(p kb) (m cb) -> p kb m cb", kb=BLOCKS, cb=BLOCKS))
         tokens = held.tile([P, BLOCKS, N], BF16, name="tokens")
         x_blocks = x.rearrange("(p kb) n -> p kb n", kb=BLOCKS)
-        gate_b = held.tile([P, BLOCKS], F32, name="gate_b")
-        for piece, cols in enumerate(PIECE_COLS):
+        for cols in PIECE_COLS:
             nc.sync.dma_start(tokens[:, :, cols], x_blocks[:, :, cols])
-            if piece == 0:
-                nc.sync.dma_start(gate_b[:], b_gate.rearrange("(p cb) o -> p (cb o)", cb=BLOCKS))
         filter_w = held.tile([P, BLOCKS, P, BLOCKS], BF16, name="filter_w")
         nc.sync.dma_start(filter_w[:], w_filter.rearrange("(p kb) (m cb) -> p kb m cb", kb=BLOCKS, cb=BLOCKS))
         offsets = held.tile([P, N // 16], U16, name="offsets")
         nc.sync.dma_start(offsets[:], offs)
-        filter_b = held.tile([P, BLOCKS], F32, name="filter_b")
-        nc.sync.dma_start(filter_b[:], b_filter.rearrange("(p cb) o -> p (cb o)", cb=BLOCKS))
         base_blocks = base.rearrange("(p cb) s -> p cb s", cb=BLOCKS)
         out_blocks = out.rearrange("(p cb) s -> p cb s", cb=BLOCKS)
         windows = []

@@ -29,7 +29,7 @@ def tile_opengrammarmodel_kernel(tc, base, x, w_gate, b_gate, w_filter, b_filter
     with (
         tc.tile_pool(name="held", bufs=1) as held,
         tc.tile_pool(name="turn", bufs=1) as turn,
-        tc.psum_pool(name="psum", bufs=3) as psum,
+        tc.psum_pool(name="psum", bufs=7) as psum,
         tc.psum_pool(name="once", bufs=1) as once,
     ):
         gate_b = held.tile([P, BLOCKS], F32, name="gate_b")
@@ -70,7 +70,7 @@ def tile_opengrammarmodel_kernel(tc, base, x, w_gate, b_gate, w_filter, b_filter
         for cols in PIECE_COLS:
             width = cols.stop - cols.start
             for cb in range(BLOCKS):
-                gate_ps = psum.tile([P, PIECE], F32, name="gate_ps")
+                gate_ps = psum.tile([P, PIECE], F32, name="gate_ps", tag="product")
                 for kb in range(BLOCKS):
                     nc.tensor.matmul(
                         gate_ps[:, 0:width],
@@ -95,7 +95,7 @@ def tile_opengrammarmodel_kernel(tc, base, x, w_gate, b_gate, w_filter, b_filter
             noise = turn.tile([P, N], F32, name="noise")
             for cols in PIECE_COLS:
                 width = cols.stop - cols.start
-                noise_ps = psum.tile([P, PIECE], F32, name="noise_ps")
+                noise_ps = psum.tile([P, PIECE], F32, name="noise_ps", tag="product")
                 for kb in range(BLOCKS):
                     nc.tensor.matmul(
                         noise_ps[:, 0:width],

@@ -84,11 +84,11 @@ def tile_opengrammarmodel_kernel(tc, base, x, w_gate, b_gate, w_filter, b_filter
                     x1_bf[:, cb, cols], gate[:, cb, cols], 1.0 / DOPAMINE, amplified[:, cb, cols], ADD, MULT
                 )
         x1 = held.tile([P, BLOCKS, N], F32, name="x1")
-        for cb in range(BLOCKS):
-            for cols in PIECE_COLS:
-                nc.vector.scalar_tensor_tensor(
-                    x1[:, cb, cols], gate[:, cb, cols], 1.0 / DOPAMINE, amplified[:, cb, cols], ADD, MULT
-                )
+        for cols in PIECE_COLS:
+            nc.vector.scalar_tensor_tensor(
+                x1[:, 0, cols], gate[:, 0, cols], 1.0 / DOPAMINE, amplified[:, 0, cols], ADD, MULT
+            )
+        nc.vector.scalar_tensor_tensor(x1[:, 1, :], gate[:, 1, :], 1.0 / DOPAMINE, amplified[:, 1, :], ADD, MULT)
 
         half_noise = held.tile([P, BLOCKS, N], F32, name="half_noise")
         for cb in range(BLOCKS):

@@ -16,7 +16,7 @@ BLOCKS = C // P
 PIECE = 256
 WIDTHS = [PIECE // 2] + (N // PIECE - 1) * [PIECE] + [PIECE // 2]
 PIECE_COLS = [slice(sum(WIDTHS[:piece]), sum(WIDTHS[: piece + 1])) for piece in range(len(WIDTHS))]
-WARM_MATMULS = 14
+WARM_MATMULS = 9
 
 DOPAMINE = 0.75
 NORADRENALINE = 0.5

@@ -16,6 +16,7 @@ BLOCKS = C // P
 PIECE = 256
 WIDTHS = [PIECE // 2] + (N // PIECE - 1) * [PIECE] + [PIECE // 2]
 PIECE_COLS = [slice(sum(WIDTHS[:piece]), sum(WIDTHS[: piece + 1])) for piece in range(len(WIDTHS))]
+LOAD_COLS = [slice(0, N // 4), slice(N // 4, N // 2), slice(N // 2, N)]
 WARM_MATMULS = 9
 
 DOPAMINE = 0.75
@@ -37,10 +38,10 @@ def tile_opengrammarmodel_kernel(tc, base, x, w_gate, b_gate, w_filter, b_filter
         filter_b = held.tile([P, BLOCKS], F32, name="filter_b")
         nc.scalar.dma_start(filter_b[:], b_filter.rearrange("(p cb) o -> p (cb o)", cb=BLOCKS))
         gate_w = held.tile([P, BLOCKS, P, BLOCKS], BF16, name="gate_w")
-        nc.sync.dma_start(gate_w[:], w_gate.rearrange("(p kb) (m cb) -> p kb m cb", kb=BLOCKS, cb=BLOCKS))
         tokens = held.tile([P, BLOCKS, N], BF16, name="tokens")
         x_blocks = x.rearrange("(p kb) n -> p kb n", kb=BLOCKS)
-        for cols in PIECE_COLS:
+        nc.sync.dma_start(gate_w[:], w_gate.rearrange("(p kb) (m cb) -> p kb m cb", kb=BLOCKS, cb=BLOCKS))
+        for cols in LOAD_COLS:
             nc.sync.dma_start(tokens[:, :, cols], x_blocks[:, :, cols])
         filter_w = held.tile([P, BLOCKS, P, BLOCKS], BF16, name="filter_w")
         nc.sync.dma_start(filter_w[:], w_filter.rearrange("(p kb) (m cb) -> p kb m cb", kb=BLOCKS, cb=BLOCKS))
@@ -63,7 +64,7 @@ def tile_opengrammarmodel_kernel(tc, base, x, w_gate, b_gate, w_filter, b_filter
         nc.scalar.activation(warm_gate[:], zeros[:, 0:1], SIGMOID)
 
         amplified = held.tile([P, BLOCKS, N], F32, name="amplified")
-        for cols in PIECE_COLS:
+        for cols in LOAD_COLS:
             nc.vector.tensor_scalar_mul(amplified[:, :, cols], tokens[:, :, cols], DOPAMINE)
         gate = held.tile([P, BLOCKS, N], F32, name="gate")
         x1_bf = held.tile([P, BLOCKS, N], BF16, name="x1_bf")

@@ -45,8 +45,6 @@ def tile_opengrammarmodel_kernel(tc, base, x, w_gate, b_gate, w_filter, b_filter
             nc.sync.dma_start(tokens[:, :, cols], x_blocks[:, :, cols])
         filter_w = held.tile([P, BLOCKS, P, BLOCKS], BF16, name="filter_w")
         nc.sync.dma_start(filter_w[:], w_filter.rearrange("(p kb) (m cb) -> p kb m cb", kb=BLOCKS, cb=BLOCKS))
-        offsets = held.tile([P, N // 16], U16, name="offsets")
-        nc.sync.dma_start(offsets[:], offs)
         base_blocks = base.rearrange("(p cb) s -> p cb s", cb=BLOCKS)
         out_blocks = out.rearrange("(p cb) s -> p cb s", cb=BLOCKS)
         windows = []
@@ -54,6 +52,9 @@ def tile_opengrammarmodel_kernel(tc, base, x, w_gate, b_gate, w_filter, b_filter
             window = held.tile([P, S], F32, name=f"window{cb}")
             nc.sync.dma_start(window[:], base_blocks[:, cb, :])
             windows.append(window)
+            if cb == 0:
+                offsets = held.tile([P, N // 16], U16, name="offsets")
+                nc.sync.dma_start(offsets[:], offs)
 
         zeros = held.tile([P, P], BF16, name="zeros")
         nc.vector.memset(zeros[:], 0.0)
@@ -94,7 +95,7 @@ def tile_opengrammarmodel_kernel(tc, base, x, w_gate, b_gate, w_filter, b_filter
         half_noise = held.tile([P, BLOCKS, N], F32, name="half_noise")
         for cb in range(BLOCKS):
             noise = turn.tile([P, N], F32, name="noise")
-            for cols in PIECE_COLS:
+            for piece, cols in enumerate(PIECE_COLS):
                 width = cols.stop - cols.start
                 noise_ps = psum.tile([P, PIECE], F32, name="noise_ps", tag="product")
                 for kb in range(BLOCKS):
@@ -106,7 +107,10 @@ def tile_opengrammarmodel_kernel(tc, base, x, w_gate, b_gate, w_filter, b_filter
                         stop=(kb == BLOCKS - 1),
                     )
                 nc.scalar.activation(noise[:, cols], noise_ps[:, 0:width], TANH, bias=filter_b[:, cb : cb + 1])
-                nc.scalar.mul(half_noise[:, cb, cols], noise[:, cols], NORADRENALINE)
+                if piece > 0:
+                    before = PIECE_COLS[piece - 1]
+                    nc.scalar.mul(half_noise[:, cb, before], noise[:, before], NORADRENALINE)
+            nc.scalar.mul(half_noise[:, cb, PIECE_COLS[-1]], noise[:, PIECE_COLS[-1]], NORADRENALINE)
             nc.vector.tensor_tensor(windows[cb][:].indirect(offsets[:]), x1[:, cb, :], half_noise[:, cb, :], ADD)
             nc.sync.dma_start(out_blocks[:, cb, 0 : S // 2], windows[cb][:, 0 : S // 2])
             nc.scalar.dma_start(out_blocks[:, cb, S // 2 : S], windows[cb][:, S // 2 : S])

import concourse.mybir as mybir

F32 = mybir.dt.float32
BF16 = mybir.dt.bfloat16
U16 = mybir.dt.uint16
ADD = mybir.AluOpType.add
MULT = mybir.AluOpType.mult
SIGMOID = mybir.ActivationFunctionType.Sigmoid
TANH = mybir.ActivationFunctionType.Tanh

P = 128
C = 256
S = 4096
N = 1024
BLOCKS = C // P
PIECE = 256
WIDTHS = [PIECE // 2] + (N // PIECE - 1) * [PIECE] + [PIECE // 2]
PIECE_COLS = [slice(sum(WIDTHS[:piece]), sum(WIDTHS[: piece + 1])) for piece in range(len(WIDTHS))]
LOAD_COLS = [slice(0, N // 4), slice(N // 4, N // 2), slice(N // 2, N)]
WARM_MATMULS = 9

DOPAMINE = 0.75
NORADRENALINE = 0.5

FLOPS = 2 * 2 * C * C * N


def tile_opengrammarmodel_kernel(tc, base, x, w_gate, b_gate, w_filter, b_filter, offs, out):
    nc = tc.nc
    with (
        tc.tile_pool(name="held", bufs=1) as held,
        tc.tile_pool(name="turn", bufs=1) as turn,
        tc.psum_pool(name="psum", bufs=7) as psum,
        tc.psum_pool(name="once", bufs=1) as once,
    ):
        gate_b = held.tile([P, BLOCKS], F32, name="gate_b")
        nc.scalar.dma_start(gate_b[:], b_gate.rearrange("(p cb) o -> p (cb o)", cb=BLOCKS))
        filter_b = held.tile([P, BLOCKS], F32, name="filter_b")
        nc.scalar.dma_start(filter_b[:], b_filter.rearrange("(p cb) o -> p (cb o)", cb=BLOCKS))
        gate_w = held.tile([P, BLOCKS, P, BLOCKS], BF16, name="gate_w")
        tokens = held.tile([P, BLOCKS, N], BF16, name="tokens")
        x_blocks = x.rearrange("(p kb) n -> p kb n", kb=BLOCKS)
        nc.sync.dma_start(gate_w[:], w_gate.rearrange("(p kb) (m cb) -> p kb m cb", kb=BLOCKS, cb=BLOCKS))
        for cols in LOAD_COLS:
            nc.sync.dma_start(tokens[:, :, cols], x_blocks[:, :, cols])
        filter_w = held.tile([P, BLOCKS, P, BLOCKS], BF16, name="filter_w")
        nc.sync.dma_start(filter_w[:], w_filter.rearrange("(p kb) (m cb) -> p kb m cb", kb=BLOCKS, cb=BLOCKS))
        base_blocks = base.rearrange("(p cb) s -> p cb s", cb=BLOCKS)
        out_blocks = out.rearrange("(p cb) s -> p cb s", cb=BLOCKS)
        windows = []
        for cb in range(BLOCKS):
            window = held.tile([P, S], F32, name=f"window{cb}")
            nc.sync.dma_start(window[:], base_blocks[:, cb, :])
            windows.append(window)
            if cb == 0:
                offsets = held.tile([P, N // 16], U16, name="offsets")
                nc.sync.dma_start(offsets[:], offs)

        zeros = held.tile([P, P], BF16, name="zeros")
        nc.vector.memset(zeros[:], 0.0)
        warm_ps = once.tile([P, P], F32, name="warm_ps")
        for rep in range(WARM_MATMULS):
            nc.tensor.matmul(warm_ps[:], zeros[:], zeros[:], start=True, stop=True)
        warm_gate = held.tile([P, 1], F32, name="warm_gate")
        nc.scalar.activation(warm_gate[:], zeros[:, 0:1], SIGMOID)

        amplified = held.tile([P, BLOCKS, N], F32, name="amplified")
        for cols in LOAD_COLS:
            nc.vector.tensor_scalar_mul(amplified[:, :, cols], tokens[:, :, cols], DOPAMINE)
        gate = held.tile([P, BLOCKS, N], F32, name="gate")
        x1_bf = held.tile([P, BLOCKS, N], BF16, name="x1_bf")
        for cols in PIECE_COLS:
            width = cols.stop - cols.start
            for cb in range(BLOCKS):
                gate_ps = psum.tile([P, PIECE], F32, name="gate_ps", tag="product")
                for kb in range(BLOCKS):
                    nc.tensor.matmul(
                        gate_ps[:, 0:width],
                        gate_w[:, kb, :, cb],
                        tokens[:, kb, cols],
                        start=(kb == 0),
                        stop=(kb == BLOCKS - 1),
                    )
                nc.scalar.activation(gate[:, cb, cols], gate_ps[:, 0:width], SIGMOID, bias=gate_b[:, cb : cb + 1])
                nc.vector.scalar_tensor_tensor(
                    x1_bf[:, cb, cols], gate[:, cb, cols], 1.0 / DOPAMINE, amplified[:, cb, cols], ADD, MULT
                )
        x1 = held.tile([P, BLOCKS, N], F32, name="x1")
        for cols in PIECE_COLS:
            nc.vector.scalar_tensor_tensor(
                x1[:, 0, cols], gate[:, 0, cols], 1.0 / DOPAMINE, amplified[:, 0, cols], ADD, MULT
            )
        nc.vector.scalar_tensor_tensor(x1[:, 1, :], gate[:, 1, :], 1.0 / DOPAMINE, amplified[:, 1, :], ADD, MULT)

        half_noise = held.tile([P, BLOCKS, N], F32, name="half_noise")
        for cb in range(BLOCKS):
            noise = turn.tile([P, N], F32, name="noise")
            for piece, cols in enumerate(PIECE_COLS):
                width = cols.stop - cols.start
                noise_ps = psum.tile([P, PIECE], F32, name="noise_ps", tag="product")
                for kb in range(BLOCKS):
                    nc.tensor.matmul(
                        noise_ps[:, 0:width],
                        filter_w[:, kb, :, cb],
                        x1_bf[:, kb, cols],
                        start=(kb == 0),
                        stop=(kb == BLOCKS - 1),
                    )
                nc.scalar.activation(noise[:, cols], noise_ps[:, 0:width], TANH, bias=filter_b[:, cb : cb + 1])
                if piece > 0:
                    before = PIECE_COLS[piece - 1]
                    nc.scalar.mul(half_noise[:, cb, before], noise[:, before], NORADRENALINE)
            nc.scalar.mul(half_noise[:, cb, PIECE_COLS[-1]], noise[:, PIECE_COLS[-1]], NORADRENALINE)
            nc.vector.tensor_tensor(windows[cb][:].indirect(offsets[:]), x1[:, cb, :], half_noise[:, cb, :], ADD)
            nc.sync.dma_start(out_blocks[:, cb, 0 : S // 2], windows[cb][:, 0 : S // 2])
            nc.scalar.dma_start(out_blocks[:, cb, S // 2 : S], windows[cb][:, S // 2 : S])
